import numpy as np
import ml_dtypes


def mxq(x, axis, fmt="e4m3"):
    dtype, down = {"e4m3": (ml_dtypes.float8_e4m3fn, 7), "e5m2": (ml_dtypes.float8_e5m2, 14)}[fmt]
    v = np.moveaxis(np.asarray(x, np.float32).astype(ml_dtypes.bfloat16).astype(np.float64), axis, -1)
    blocks = v.reshape(v.shape[:-1] + (-1, 32))
    amax = np.abs(blocks).max(-1, keepdims=True)
    byte = np.maximum(np.where(amax > 0, np.frexp(amax)[1] - 1 + 127, 0) - down, 1)
    scale = np.exp2(byte - 127.0)
    codes = (blocks / scale).astype(np.float32).astype(dtype).astype(np.float64)
    return np.moveaxis((codes * scale).reshape(v.shape), -1, axis)


WIDE = False


def mx_kscale(k):
    if not WIDE:
        return np.ones(k)
    levels = np.array([20, -20, 10, -10, 0])
    a = np.random.permutation(np.resize(levels, k // 512 * 4)).reshape(k // 512, 4)
    idx = np.arange(k)
    return np.exp2(a[idx // 512, idx % 128 // 32])


BF16 = ml_dtypes.bfloat16


def bf(x):
    return np.asarray(x, np.float32).astype(BF16)


def f64(x):
    return np.asarray(x).astype(np.float64)


B, S = 4, 128
IN_FEATURES = 4096
OUT_FEATURES = 2048
GROUP_SIZE = 128
GROUPS_PER_ROW = IN_FEATURES // GROUP_SIZE
NUM_GROUPS = OUT_FEATURES * IN_FEATURES // GROUP_SIZE


def dequant(weight_q, weight_scale, weight_zero_point):
    w = f64(weight_q).reshape(-1, GROUP_SIZE)
    w = (w - f64(weight_zero_point)) * f64(weight_scale)
    return w.reshape(OUT_FEATURES, IN_FEATURES)


def setup_inputs():
    u = mx_kscale(OUT_FEATURES)
    x = np.random.standard_normal((B, S, IN_FEATURES))
    wq = np.random.randint(0, 16, (OUT_FEATURES, IN_FEATURES)).astype(np.float64)
    sc = np.random.uniform(0.001, 0.004, (OUT_FEATURES, GROUPS_PER_ROW)) / u[:, None]
    zp = np.random.randint(0, 16, (NUM_GROUPS, 1)).astype(np.float64)
    g = np.random.standard_normal((B, S, OUT_FEATURES)) * np.exp2(np.random.randint(-12, 1, (B, S, 1))) * 8.0 * u
    return {"input": bf(x), "weight_q": bf(wq), "weight_scale": bf(sc.reshape(NUM_GROUPS, 1)), "weight_zero_point": bf(zp), "grad_out": bf(g)}


def reference(input, weight_q, weight_scale, weight_zero_point, grad_out):
    w = dequant(weight_q, weight_scale, weight_zero_point)
    return mxq(f64(grad_out), 2, "e5m2") @ mxq(w, 0, "e4m3")

@@ -1,0 +1,179 @@
+from contextlib import ExitStack
+
+import concourse.mybir as mybir
+from concourse.masks import make_identity
+
+F32 = mybir.dt.float32
+BF16 = mybir.dt.bfloat16
+U32 = mybir.dt.uint32
+U8 = mybir.dt.uint8
+E4M3X4 = mybir.dt.float8_e4m3fn_x4
+E5M2X4 = mybir.dt.float8_e5m2_x4
+ALU = mybir.AluOpType
+
+P = 128
+PACK = 4
+K_PASS = P * PACK
+TOKENS = 512
+OUT_F = 2048
+IN_F = 4096
+GROUP = 128
+GROUPS_PER_ROW = IN_F // GROUP
+N_TT = TOKENS // P
+N_C = OUT_F // K_PASS
+BLOCK = 1024
+HALF = 512
+N_BLOCKS = IN_F // BLOCK
+V_COLS = 192
+
+FLOPS = 2 * TOKENS * OUT_F * IN_F
+BYTES = 2 * OUT_F * IN_F + 2 * 2 * OUT_F * GROUPS_PER_ROW + 2 * TOKENS * OUT_F + 4 * TOKENS * IN_F
+
+
+def tile_qlv4_linear_mod_kernel(
+    tc, x_in, weight_q, weight_scale, weight_zero_point, grad_out, out
+):
+    nc = tc.nc
+    g2 = grad_out.flatten_outer_dims()
+    out2 = out.flatten_outer_dims()
+    wq_v = weight_q.rearrange("(c p j) i -> c p j i", p=P, j=PACK)
+    sc_v = weight_scale.rearrange("(c p r) one -> p c (r one)", c=N_C, p=P)
+    zp_v = weight_zero_point.rearrange("(c p r) one -> p c (r one)", c=N_C, p=P)
+
+    with ExitStack() as ctx:
+        const = ctx.enter_context(tc.tile_pool(name="const", bufs=1))
+        wpool = ctx.enter_context(tc.tile_pool(name="wq", bufs=8))
+        gpool = ctx.enter_context(tc.tile_pool(name="grouped", bufs=4))
+        cpool = ctx.enter_context(tc.tile_pool(name="codes", bufs=16))
+        epool = ctx.enter_context(tc.tile_pool(name="ev", bufs=8))
+        qpool = ctx.enter_context(tc.tile_pool(name="gq", bufs=3))
+        psum = ctx.enter_context(tc.psum_pool(name="psum", bufs=8))
+
+        zp_bf = const.tile([P, N_C, P], BF16)
+        sc_bf = const.tile([P, N_C, P], BF16)
+        nc.sync.dma_start(out=zp_bf[:], in_=zp_v)
+        nc.sync.dma_start(out=sc_bf[:], in_=sc_v)
+
+        w_tiles = {}
+
+        def load_w(blk, c, pieces):
+            wt = wpool.tile([P, PACK, BLOCK], BF16, name="wt")
+            w_tiles[(blk, c)] = wt
+            step = BLOCK // pieces
+            for s in range(pieces):
+                nc.sync.dma_start(
+                    out=wt[:, :, s * step : (s + 1) * step],
+                    in_=wq_v[c][:, :, blk * BLOCK + s * step : blk * BLOCK + (s + 1) * step],
+                )
+
+        load_w(0, 0, 2)
+        load_w(0, 1, 1)
+        load_w(0, 2, 1)
+        g_sb = []
+        for tt in range(N_TT):
+            g_t = const.tile([P, OUT_F], BF16, name="g_sb%d" % tt)
+            nc.sync.dma_start(out=g_t[:], in_=g2[tt * P : (tt + 1) * P, :])
+            g_sb.append(g_t)
+        load_w(0, 3, 1)
+        for c in range(N_C):
+            load_w(1, c, 1)
+
+        ident = const.tile([P, P], F32)
+        make_identity(nc, ident[:])
+        zp32 = const.tile([P, N_C * P], F32)
+        sc32 = const.tile([P, N_C * P], F32)
+        nc.vector.tensor_copy(out=zp32[:], in_=zp_bf[:].rearrange("p c r -> p (c r)"))
+        nc.vector.tensor_copy(out=sc32[:], in_=sc_bf[:].rearrange("p c r -> p (c r)"))
+
+        g_codes = const.tile([P, N_TT * N_C * P], U32, align_bytes=64)
+        g_scales = const.tile([P, N_TT * N_C * P], U8, align_bytes=64)
+        for tt in range(N_TT):
+            gw = g_sb[tt][:].bitcast(F32).rearrange("p (c m u) -> p c u m", c=N_C, u=2)
+            for ch in range(2):
+                xt = psum.tile([P, HALF], F32, name="xt", tag="acc")
+                xt_v = xt[:].rearrange("p (a u t) -> p a u t", a=2, u=2)
+                for a in range(2):
+                    for u in range(2):
+                        nc.tensor.transpose(xt_v[:, a, u, :], gw[:, 2 * ch + a, u, :], ident[:])
+                gq = qpool.tile([P, 2 * K_PASS], BF16, name="gq", align_bytes=64)
+                nc.scalar.copy(
+                    out=gq[:].bitcast(F32).rearrange("p (a t u) -> p a t u", a=2, u=2),
+                    in_=xt[:].rearrange("p (a u t) -> p a t u", a=2, u=2),
+                )
+                lo = (tt * N_C + 2 * ch) * P
+                nc.vector.quantize_mx(
+                    out=g_codes[:, lo : lo + 2 * P].bitcast(E5M2X4),
+                    scales=g_scales[:, lo : lo + 2 * P],
+                    in_=gq[:],
+                )
+
+        for blk in range(N_BLOCKS):
+            last = blk == N_BLOCKS - 1
+            acc = {}
+            for c in range(N_C):
+                wt = w_tiles[(blk, c)]
+                for h in range(2):
+                    base = h * HALF
+                    for j in range(PACK):
+                        for gg in range(HALF // GROUP):
+                            col = base + gg * GROUP
+                            k = c * P + j * GROUPS_PER_ROW + (blk * BLOCK + col) // GROUP
+                            nc.vector.tensor_scalar(
+                                out=wt[:, j, col : col + GROUP],
+                                in0=wt[:, j, col : col + GROUP],
+                                scalar1=zp32[:, k : k + 1],
+                                scalar2=sc32[:, k : k + 1],
+                                op0=ALU.subtract,
+                                op1=ALU.mult,
+                            )
+                    grouped = gpool.tile([P, HALF, PACK], BF16, name="grouped", align_bytes=64)
+                    nc.vector.tensor_copy(
+                        out=grouped[:, 0:V_COLS, :].rearrange("p (q i) t -> p q t i", i=4),
+                        in_=wt[:, :, base : base + V_COLS].rearrange("p t (q i) -> p q t i", i=4),
+                    )
+                    nc.scalar.copy(
+                        out=grouped[:, V_COLS:HALF, :].rearrange("p (q i) t -> p q t i", i=4),
+                        in_=wt[:, :, base + V_COLS : base + HALF].rearrange("p t (q i) -> p q t i", i=4),
+                    )
+                    codes = cpool.tile([P, HALF], U32, name="codes", align_bytes=64)
+                    scales = cpool.tile([P, HALF], U8, name="scales", align_bytes=64)
+                    nc.vector.quantize_mx(
+                        out=codes[:].bitcast(E4M3X4),
+                        scales=scales[:],
+                        in_=grouped[:].rearrange("p w t -> p (w t)"),
+                    )
+                    for tt in range(N_TT):
+                        if c == 0:
+                            acc[(tt, h)] = psum.tile([P, HALF], F32, name="acc", tag="acc")
+                        lo = (tt * N_C + c) * P
+                        nc.tensor.matmul_mx(
+                            out=acc[(tt, h)][:],
+                            lhsT=g_codes[:, lo : lo + P].bitcast(E5M2X4),
+                            lhsT_scale=g_scales[:, lo : lo + P],
+                            rhs=codes[:].bitcast(E4M3X4),
+                            rhs_scale=scales[:],
+                            start=(c == 0),
+                            stop=(c == N_C - 1),
+                        )
+                if blk + 2 < N_BLOCKS:
+                    load_w(blk + 2, c, 1)
+            if not last:
+                for tt in range(N_TT):
+                    ev = epool.tile([P, BLOCK], F32, name="ev")
+                    for h in range(2):
+                        nc.scalar.copy(out=ev[:, h * HALF : (h + 1) * HALF], in_=acc[(tt, h)][:])
+                    nc.sync.dma_start(
+                        out=out2[tt * P : (tt + 1) * P, blk * BLOCK : (blk + 1) * BLOCK], in_=ev[:]
+                    )
+            else:
+                for h in range(2):
+                    for tt in range(N_TT):
+                        ev = epool.tile([P, HALF], F32, name="ev")
+                        if h == 1 and tt < 3:
+                            nc.vector.tensor_copy(out=ev[:], in_=acc[(tt, h)][:])
+                        else:
+                            nc.scalar.copy(out=ev[:], in_=acc[(tt, h)][:])
+                        lo = blk * BLOCK + h * HALF
+                        nc.sync.dma_start(
+                            out=out2[tt * P : (tt + 1) * P, lo : lo + HALF], in_=ev[:]
+                        )

@@ -24,7 +24,7 @@ N_C = OUT_F // K_PASS
 BLOCK = 1024
 HALF = 512
 N_BLOCKS = IN_F // BLOCK
-V_COLS = 192
+V_COLS = 256
 
 FLOPS = 2 * TOKENS * OUT_F * IN_F
 BYTES = 2 * OUT_F * IN_F + 2 * 2 * OUT_F * GROUPS_PER_ROW + 2 * TOKENS * OUT_F + 4 * TOKENS * IN_F

@@ -24,30 +24,56 @@ N_C = OUT_F // K_PASS
 BLOCK = 1024
 HALF = 512
 N_BLOCKS = IN_F // BLOCK
-V_COLS = 256
+N_IB = IN_F // HALF
+N_UNITS = N_IB * N_C
+W_RING = 8
+G_T0 = 3
+E_LAG = 3
+FIRST_EVAC_LATE = {0: 2, 1: 1}
+V_COLS = {0: 104, 1: 192, 2: 280, 3: 368}
+V_COLS_LAST = 256
 
 FLOPS = 2 * TOKENS * OUT_F * IN_F
 BYTES = 2 * OUT_F * IN_F + 2 * 2 * OUT_F * GROUPS_PER_ROW + 2 * TOKENS * OUT_F + 4 * TOKENS * IN_F
+
+
+def evac_step(ib, tt):
+    close = N_C * ib + N_C - 1
+    if ib == N_IB - 1:
+        return close + E_LAG
+    return close + E_LAG + FIRST_EVAC_LATE.get(ib, 0) + tt
 
 
 def tile_qlv4_linear_mod_kernel(
     tc, x_in, weight_q, weight_scale, weight_zero_point, grad_out, out
 ):
     nc = tc.nc
-    g2 = grad_out.flatten_outer_dims()
+    g_v = grad_out.flatten_outer_dims().rearrange("(a p) o -> p a o", p=P)
     out2 = out.flatten_outer_dims()
     wq_v = weight_q.rearrange("(c p j) i -> c p j i", p=P, j=PACK)
     sc_v = weight_scale.rearrange("(c p r) one -> p c (r one)", c=N_C, p=P)
     zp_v = weight_zero_point.rearrange("(c p r) one -> p c (r one)", c=N_C, p=P)
 
+    evac_plan = {}
+    for ib in range(N_IB):
+        for tt in range(N_TT):
+            step = evac_step(ib, tt)
+            if step not in evac_plan:
+                evac_plan[step] = []
+            evac_plan[step].append((ib, tt))
+
     with ExitStack() as ctx:
         const = ctx.enter_context(tc.tile_pool(name="const", bufs=1))
-        wpool = ctx.enter_context(tc.tile_pool(name="wq", bufs=8))
+        wpool = ctx.enter_context(tc.tile_pool(name="wq", bufs=W_RING))
         gpool = ctx.enter_context(tc.tile_pool(name="grouped", bufs=4))
-        cpool = ctx.enter_context(tc.tile_pool(name="codes", bufs=16))
+        cpool = ctx.enter_context(tc.tile_pool(name="codes", bufs=8))
         epool = ctx.enter_context(tc.tile_pool(name="ev", bufs=8))
-        qpool = ctx.enter_context(tc.tile_pool(name="gq", bufs=3))
-        psum = ctx.enter_context(tc.psum_pool(name="psum", bufs=8))
+        qpool = ctx.enter_context(tc.tile_pool(name="gq", bufs=4))
+        psum = ctx.enter_context(tc.psum_pool(name="psum", bufs=1))
+        ctx.enter_context(tc.manual_schedule())
+
+        def bank(n):
+            return psum.tile([P, HALF], F32, name="bank%d" % n, tag="bank%d" % n)
 
         zp_bf = const.tile([P, N_C, P], BF16)
         sc_bf = const.tile([P, N_C, P], BF16)
@@ -56,27 +82,28 @@ def tile_qlv4_linear_mod_kernel(
 
         w_tiles = {}
 
-        def load_w(blk, c, pieces):
-            wt = wpool.tile([P, PACK, BLOCK], BF16, name="wt")
-            w_tiles[(blk, c)] = wt
-            step = BLOCK // pieces
-            for s in range(pieces):
-                nc.sync.dma_start(
-                    out=wt[:, :, s * step : (s + 1) * step],
-                    in_=wq_v[c][:, :, blk * BLOCK + s * step : blk * BLOCK + (s + 1) * step],
-                )
+        def load_w(blk, c, lo, hi):
+            if (blk, c) not in w_tiles:
+                w_tiles[(blk, c)] = wpool.tile([P, PACK, BLOCK], BF16, name="wt")
+            nc.sync.dma_start(
+                out=w_tiles[(blk, c)][:, :, lo:hi],
+                in_=wq_v[c][:, :, blk * BLOCK + lo : blk * BLOCK + hi],
+            )
 
-        load_w(0, 0, 2)
-        load_w(0, 1, 1)
-        load_w(0, 2, 1)
         g_sb = []
-        for tt in range(N_TT):
-            g_t = const.tile([P, OUT_F], BF16, name="g_sb%d" % tt)
-            nc.sync.dma_start(out=g_t[:], in_=g2[tt * P : (tt + 1) * P, :])
-            g_sb.append(g_t)
-        load_w(0, 3, 1)
+        n = 0
+        for h in range(2):
+            for c in range(N_C):
+                load_w(0, c, h * HALF, (h + 1) * HALF)
+                if 2 <= n < 2 + N_C:
+                    g_t = const.tile([P, N_TT, K_PASS], BF16, name="g_sb%d" % (n - 2))
+                    nc.sync.dma_start(
+                        out=g_t[:], in_=g_v[:, :, (n - 2) * K_PASS : (n - 1) * K_PASS]
+                    )
+                    g_sb.append(g_t)
+                n += 1
         for c in range(N_C):
-            load_w(1, c, 1)
+            load_w(1, c, 0, BLOCK)
 
         ident = const.tile([P, P], F32)
         make_identity(nc, ident[:])
@@ -85,95 +112,142 @@ def tile_qlv4_linear_mod_kernel(
         nc.vector.tensor_copy(out=zp32[:], in_=zp_bf[:].rearrange("p c r -> p (c r)"))
         nc.vector.tensor_copy(out=sc32[:], in_=sc_bf[:].rearrange("p c r -> p (c r)"))
 
-        g_codes = const.tile([P, N_TT * N_C * P], U32, align_bytes=64)
-        g_scales = const.tile([P, N_TT * N_C * P], U8, align_bytes=64)
-        for tt in range(N_TT):
-            gw = g_sb[tt][:].bitcast(F32).rearrange("p (c m u) -> p c u m", c=N_C, u=2)
-            for ch in range(2):
-                xt = psum.tile([P, HALF], F32, name="xt", tag="acc")
+        g_codes = const.tile([P, N_C * N_TT * P], U32, align_bytes=64)
+        g_scales = const.tile([P, N_C * N_TT * P], U8, align_bytes=64)
+
+        grouped_of = {}
+        codes_of = {}
+        gq_of = {}
+        acc = {}
+        state = {"g_ready": 0, "multiplied": 0}
+        evacuated = {}
+        pending = []
+
+        def where(u):
+            ib = u // N_C
+            return ib, u % N_C, ib // 2, ib % 2
+
+        def dequantise(u):
+            ib, c, blk, h = where(u)
+            wt = w_tiles[(blk, c)]
+            for j in range(PACK):
+                for gg in range(HALF // GROUP):
+                    col = h * HALF + gg * GROUP
+                    k = c * P + j * GROUPS_PER_ROW + (blk * BLOCK + col) // GROUP
+                    nc.vector.tensor_scalar(
+                        out=wt[:, j, col : col + GROUP],
+                        in0=wt[:, j, col : col + GROUP],
+                        scalar1=zp32[:, k : k + 1],
+                        scalar2=sc32[:, k : k + 1],
+                        op0=ALU.subtract,
+                        op1=ALU.mult,
+                    )
+
+        def regroup(u, v_cols):
+            ib, c, blk, h = where(u)
+            wt = w_tiles[(blk, c)]
+            base = h * HALF
+            grouped = gpool.tile([P, HALF, PACK], BF16, name="grouped", align_bytes=64)
+            grouped_of[u] = grouped
+            nc.vector.tensor_copy(
+                out=grouped[:, 0:v_cols, :].rearrange("p (q i) t -> p q t i", i=4),
+                in_=wt[:, :, base : base + v_cols].rearrange("p t (q i) -> p q t i", i=4),
+            )
+            nc.scalar.copy(
+                out=grouped[:, v_cols:HALF, :].rearrange("p (q i) t -> p q t i", i=4),
+                in_=wt[:, :, base + v_cols : base + HALF].rearrange("p t (q i) -> p q t i", i=4),
+            )
+            if h == 1 and blk + 2 < N_BLOCKS:
+                load_w(blk + 2, c, 0, BLOCK)
+
+        def quantise(u):
+            codes = cpool.tile([P, HALF], U32, name="codes", align_bytes=64)
+            scales = cpool.tile([P, HALF], U8, name="scales", align_bytes=64)
+            codes_of[u] = (codes, scales)
+            nc.vector.quantize_mx(
+                out=codes[:].bitcast(E4M3X4),
+                scales=scales[:],
+                in_=grouped_of[u][:].rearrange("p w t -> p (w t)"),
+            )
+            pending.append(u)
+
+        def multiply_what_can_go():
+            while state["multiplied"] < len(pending):
+                u = pending[state["multiplied"]]
+                ib, c, blk, h = where(u)
+                if c >= state["g_ready"]:
+                    return
+                if c == 0 and ib >= 2 and evacuated.get(ib - 2, 0) < N_TT:
+                    return
+                state["multiplied"] += 1
+                codes, scales = codes_of[u]
+                for tt in range(N_TT):
+                    if c == 0:
+                        acc[(ib, tt)] = bank((ib % 2) * N_TT + tt)
+                    lo = (c * N_TT + tt) * P
+                    nc.tensor.matmul_mx(
+                        out=acc[(ib, tt)][:],
+                        lhsT=g_codes[:, lo : lo + P].bitcast(E5M2X4),
+                        lhsT_scale=g_scales[:, lo : lo + P],
+                        rhs=codes[:].bitcast(E4M3X4),
+                        rhs_scale=scales[:],
+                        start=(c == 0),
+                        stop=(c == N_C - 1),
+                    )
+
+        def g_transpose(c):
+            for k in range(2):
+                xt = bank(N_TT + (2 * c + k) % N_TT)
                 xt_v = xt[:].rearrange("p (a u t) -> p a u t", a=2, u=2)
                 for a in range(2):
+                    gw = g_sb[c][:, 2 * k + a, :].bitcast(F32).rearrange("p (m u) -> p u m", u=2)
                     for u in range(2):
-                        nc.tensor.transpose(xt_v[:, a, u, :], gw[:, 2 * ch + a, u, :], ident[:])
+                        nc.tensor.transpose(xt_v[:, a, u, :], gw[:, u, :], ident[:])
                 gq = qpool.tile([P, 2 * K_PASS], BF16, name="gq", align_bytes=64)
+                gq_of[(c, k)] = gq
                 nc.scalar.copy(
                     out=gq[:].bitcast(F32).rearrange("p (a t u) -> p a t u", a=2, u=2),
                     in_=xt[:].rearrange("p (a u t) -> p a t u", a=2, u=2),
                 )
-                lo = (tt * N_C + 2 * ch) * P
+
+        def g_quantise(c):
+            for k in range(2):
+                lo = (c * N_TT + 2 * k) * P
                 nc.vector.quantize_mx(
                     out=g_codes[:, lo : lo + 2 * P].bitcast(E5M2X4),
                     scales=g_scales[:, lo : lo + 2 * P],
-                    in_=gq[:],
+                    in_=gq_of[(c, k)][:],
                 )
+            state["g_ready"] = c + 1
 
-        for blk in range(N_BLOCKS):
-            last = blk == N_BLOCKS - 1
-            acc = {}
-            for c in range(N_C):
-                wt = w_tiles[(blk, c)]
-                for h in range(2):
-                    base = h * HALF
-                    for j in range(PACK):
-                        for gg in range(HALF // GROUP):
-                            col = base + gg * GROUP
-                            k = c * P + j * GROUPS_PER_ROW + (blk * BLOCK + col) // GROUP
-                            nc.vector.tensor_scalar(
-                                out=wt[:, j, col : col + GROUP],
-                                in0=wt[:, j, col : col + GROUP],
-                                scalar1=zp32[:, k : k + 1],
-                                scalar2=sc32[:, k : k + 1],
-                                op0=ALU.subtract,
-                                op1=ALU.mult,
-                            )
-                    grouped = gpool.tile([P, HALF, PACK], BF16, name="grouped", align_bytes=64)
-                    nc.vector.tensor_copy(
-                        out=grouped[:, 0:V_COLS, :].rearrange("p (q i) t -> p q t i", i=4),
-                        in_=wt[:, :, base : base + V_COLS].rearrange("p t (q i) -> p q t i", i=4),
-                    )
-                    nc.scalar.copy(
-                        out=grouped[:, V_COLS:HALF, :].rearrange("p (q i) t -> p q t i", i=4),
-                        in_=wt[:, :, base + V_COLS : base + HALF].rearrange("p t (q i) -> p q t i", i=4),
-                    )
-                    codes = cpool.tile([P, HALF], U32, name="codes", align_bytes=64)
-                    scales = cpool.tile([P, HALF], U8, name="scales", align_bytes=64)
-                    nc.vector.quantize_mx(
-                        out=codes[:].bitcast(E4M3X4),
-                        scales=scales[:],
-                        in_=grouped[:].rearrange("p w t -> p (w t)"),
-                    )
-                    for tt in range(N_TT):
-                        if c == 0:
-                            acc[(tt, h)] = psum.tile([P, HALF], F32, name="acc", tag="acc")
-                        lo = (tt * N_C + c) * P
-                        nc.tensor.matmul_mx(
-                            out=acc[(tt, h)][:],
-                            lhsT=g_codes[:, lo : lo + P].bitcast(E5M2X4),
-                            lhsT_scale=g_scales[:, lo : lo + P],
-                            rhs=codes[:].bitcast(E4M3X4),
-                            rhs_scale=scales[:],
-                            start=(c == 0),
-                            stop=(c == N_C - 1),
-                        )
-                if blk + 2 < N_BLOCKS:
-                    load_w(blk + 2, c, 1)
-            if not last:
-                for tt in range(N_TT):
-                    ev = epool.tile([P, BLOCK], F32, name="ev")
-                    for h in range(2):
-                        nc.scalar.copy(out=ev[:, h * HALF : (h + 1) * HALF], in_=acc[(tt, h)][:])
-                    nc.sync.dma_start(
-                        out=out2[tt * P : (tt + 1) * P, blk * BLOCK : (blk + 1) * BLOCK], in_=ev[:]
-                    )
+        def evacuate(ib, tt):
+            ev = epool.tile([P, HALF], F32, name="ev")
+            if ib == N_IB - 1 and tt < 2:
+                nc.vector.tensor_copy(out=ev[:], in_=acc[(ib, tt)][:])
             else:
-                for h in range(2):
-                    for tt in range(N_TT):
-                        ev = epool.tile([P, HALF], F32, name="ev")
-                        if h == 1 and tt < 3:
-                            nc.vector.tensor_copy(out=ev[:], in_=acc[(tt, h)][:])
-                        else:
-                            nc.scalar.copy(out=ev[:], in_=acc[(tt, h)][:])
-                        lo = blk * BLOCK + h * HALF
-                        nc.sync.dma_start(
-                            out=out2[tt * P : (tt + 1) * P, lo : lo + HALF], in_=ev[:]
-                        )
+                nc.scalar.copy(out=ev[:], in_=acc[(ib, tt)][:])
+            nc.sync.dma_start(
+                out=out2[tt * P : (tt + 1) * P, ib * HALF : (ib + 1) * HALF], in_=ev[:]
+            )
+            evacuated[ib] = evacuated.get(ib, 0) + 1
+
+        for step in range(N_UNITS + E_LAG):
+            if 0 <= step - 2 < N_UNITS:
+                quantise(step - 2)
+            if 0 <= step - G_T0 - 1 < N_C:
+                g_quantise(step - G_T0 - 1)
+            multiply_what_can_go()
+            todo = evac_plan.get(step, [])
+            if 0 <= step - 1 < N_UNITS:
+                banks_for_scalar = len(todo) + (2 if 0 <= step - G_T0 < N_C else 0)
+                v_cols = V_COLS[banks_for_scalar]
+                if step - 1 == N_UNITS - 1:
+                    v_cols = V_COLS_LAST
+                regroup(step - 1, v_cols)
+            if 0 <= step - G_T0 < N_C:
+                g_transpose(step - G_T0)
+            if step < N_UNITS:
+                dequantise(step)
+            for ib, tt in todo:
+                evacuate(ib, tt)
+            multiply_what_can_go()

@@ -26,47 +26,54 @@ HALF = 512
 N_BLOCKS = IN_F // BLOCK
 N_IB = IN_F // HALF
 N_UNITS = N_IB * N_C
-W_RING = 8
-G_T0 = 3
+TILE_BY_TILE_BLOCKS = 2
+G_STEP = 5
 E_LAG = 3
-FIRST_EVAC_LATE = {0: 2, 1: 1}
-V_COLS = {0: 104, 1: 192, 2: 280, 3: 368}
+EVAC_LATE = {0: 5, 1: 3}
+V_COLS = {0: 144, 1: 224, 2: 296, 3: 376, 4: 448}
 V_COLS_LAST = 256
 
 FLOPS = 2 * TOKENS * OUT_F * IN_F
 BYTES = 2 * OUT_F * IN_F + 2 * 2 * OUT_F * GROUPS_PER_ROW + 2 * TOKENS * OUT_F + 4 * TOKENS * IN_F
 
 
-def evac_step(ib, tt):
-    close = N_C * ib + N_C - 1
-    if ib == N_IB - 1:
-        return close + E_LAG
-    return close + E_LAG + FIRST_EVAC_LATE.get(ib, 0) + tt
-
-
 def tile_qlv4_linear_mod_kernel(
     tc, x_in, weight_q, weight_scale, weight_zero_point, grad_out, out
 ):
     nc = tc.nc
-    g_v = grad_out.flatten_outer_dims().rearrange("(a p) o -> p a o", p=P)
+    g2 = grad_out.flatten_outer_dims()
     out2 = out.flatten_outer_dims()
     wq_v = weight_q.rearrange("(c p j) i -> c p j i", p=P, j=PACK)
-    sc_v = weight_scale.rearrange("(c p r) one -> p c (r one)", c=N_C, p=P)
-    zp_v = weight_zero_point.rearrange("(c p r) one -> p c (r one)", c=N_C, p=P)
+    sc_v = weight_scale.rearrange("(c p r) one -> c p (r one)", c=N_C, p=P)
+    zp_v = weight_zero_point.rearrange("(c p r) one -> c p (r one)", c=N_C, p=P)
+
+    units = []
+    for blk in range(N_BLOCKS):
+        if blk < TILE_BY_TILE_BLOCKS:
+            units.extend([(blk, c, h) for c in range(N_C) for h in range(2)])
+        else:
+            units.extend([(blk, c, h) for h in range(2) for c in range(N_C)])
 
     evac_plan = {}
     for ib in range(N_IB):
+        close = units.index((ib // 2, N_C - 1, ib % 2))
         for tt in range(N_TT):
-            step = evac_step(ib, tt)
+            if ib == N_IB - 1:
+                step = close + E_LAG
+            elif ib // 2 < TILE_BY_TILE_BLOCKS:
+                step = close + E_LAG + EVAC_LATE[ib // 2]
+            else:
+                step = close + E_LAG + tt
             if step not in evac_plan:
                 evac_plan[step] = []
             evac_plan[step].append((ib, tt))
 
     with ExitStack() as ctx:
         const = ctx.enter_context(tc.tile_pool(name="const", bufs=1))
-        wpool = ctx.enter_context(tc.tile_pool(name="wq", bufs=W_RING))
+        wpool = ctx.enter_context(tc.tile_pool(name="wq", bufs=8))
+        dpool = ctx.enter_context(tc.tile_pool(name="wd", bufs=3))
         gpool = ctx.enter_context(tc.tile_pool(name="grouped", bufs=4))
-        cpool = ctx.enter_context(tc.tile_pool(name="codes", bufs=8))
+        cpool = ctx.enter_context(tc.tile_pool(name="codes", bufs=16))
         epool = ctx.enter_context(tc.tile_pool(name="ev", bufs=8))
         qpool = ctx.enter_context(tc.tile_pool(name="gq", bufs=4))
         psum = ctx.enter_context(tc.psum_pool(name="psum", bufs=1))
@@ -75,116 +82,126 @@ def tile_qlv4_linear_mod_kernel(
         def bank(n):
             return psum.tile([P, HALF], F32, name="bank%d" % n, tag="bank%d" % n)
 
-        zp_bf = const.tile([P, N_C, P], BF16)
-        sc_bf = const.tile([P, N_C, P], BF16)
-        nc.sync.dma_start(out=zp_bf[:], in_=zp_v)
-        nc.sync.dma_start(out=sc_bf[:], in_=sc_v)
+        zp_sb = []
+        sc_sb = []
 
-        w_tiles = {}
+        def load_scalars(c):
+            zp_t = const.tile([P, P], BF16, name="zp%d" % c)
+            sc_t = const.tile([P, P], BF16, name="sc%d" % c)
+            nc.sync.dma_start(out=zp_t[:], in_=zp_v[c])
+            nc.sync.dma_start(out=sc_t[:], in_=sc_v[c])
+            zp_sb.append(zp_t)
+            sc_sb.append(sc_t)
 
-        def load_w(blk, c, lo, hi):
-            if (blk, c) not in w_tiles:
-                w_tiles[(blk, c)] = wpool.tile([P, PACK, BLOCK], BF16, name="wt")
-            nc.sync.dma_start(
-                out=w_tiles[(blk, c)][:, :, lo:hi],
-                in_=wq_v[c][:, :, blk * BLOCK + lo : blk * BLOCK + hi],
-            )
+        w_src = {}
+
+        def load_w(blk, c):
+            wt = wpool.tile([P, PACK, BLOCK], BF16, name="wt")
+            for h in range(2):
+                w_src[(blk, c, h)] = (wt, h * HALF)
+            nc.sync.dma_start(out=wt[:], in_=wq_v[c][:, :, blk * BLOCK : (blk + 1) * BLOCK])
 
         g_sb = []
-        n = 0
+
+        def load_g(tt):
+            g_t = const.tile([P, OUT_F], BF16, name="g_sb%d" % tt)
+            nc.sync.dma_start(out=g_t[:], in_=g2[tt * P : (tt + 1) * P, :])
+            g_sb.append(g_t)
+
+        load_scalars(0)
         for h in range(2):
-            for c in range(N_C):
-                load_w(0, c, h * HALF, (h + 1) * HALF)
-                if 2 <= n < 2 + N_C:
-                    g_t = const.tile([P, N_TT, K_PASS], BF16, name="g_sb%d" % (n - 2))
-                    nc.sync.dma_start(
-                        out=g_t[:], in_=g_v[:, :, (n - 2) * K_PASS : (n - 1) * K_PASS]
-                    )
-                    g_sb.append(g_t)
-                n += 1
-        for c in range(N_C):
-            load_w(1, c, 0, BLOCK)
+            first = const.tile([P, PACK, HALF], BF16, name="first%d" % h)
+            w_src[(0, 0, h)] = (first, 0)
+            nc.sync.dma_start(out=first[:], in_=wq_v[0][:, :, h * HALF : (h + 1) * HALF])
+        load_scalars(1)
+        load_w(0, 1)
+        load_scalars(2)
+        load_w(0, 2)
+        load_g(0)
+        load_g(1)
+        load_scalars(3)
+        load_w(0, 3)
+        load_g(2)
+        load_g(3)
+        later_tiles = [(blk, c) for blk in range(1, N_BLOCKS) for c in range(N_C)]
+        for blk, c in later_tiles[0:5]:
+            load_w(blk, c)
+        state = {"g_ready": 0, "multiplied": 0, "loaded": 5}
 
         ident = const.tile([P, P], F32)
         make_identity(nc, ident[:])
-        zp32 = const.tile([P, N_C * P], F32)
-        sc32 = const.tile([P, N_C * P], F32)
-        nc.vector.tensor_copy(out=zp32[:], in_=zp_bf[:].rearrange("p c r -> p (c r)"))
-        nc.vector.tensor_copy(out=sc32[:], in_=sc_bf[:].rearrange("p c r -> p (c r)"))
 
-        g_codes = const.tile([P, N_C * N_TT * P], U32, align_bytes=64)
-        g_scales = const.tile([P, N_C * N_TT * P], U8, align_bytes=64)
+        g_codes = const.tile([P, N_TT * N_C * P], U32, align_bytes=64)
+        g_scales = const.tile([P, N_TT * N_C * P], U8, align_bytes=64)
 
+        wd_of = {}
         grouped_of = {}
         codes_of = {}
         gq_of = {}
         acc = {}
-        state = {"g_ready": 0, "multiplied": 0}
         evacuated = {}
         pending = []
 
-        def where(u):
-            ib = u // N_C
-            return ib, u % N_C, ib // 2, ib % 2
-
-        def dequantise(u):
-            ib, c, blk, h = where(u)
-            wt = w_tiles[(blk, c)]
+        def dequantise(n):
+            blk, c, h = units[n]
+            wt, base = w_src[(blk, c, h)]
+            wd = dpool.tile([P, PACK, HALF], BF16, name="wd")
+            wd_of[n] = wd
             for j in range(PACK):
                 for gg in range(HALF // GROUP):
-                    col = h * HALF + gg * GROUP
-                    k = c * P + j * GROUPS_PER_ROW + (blk * BLOCK + col) // GROUP
+                    k = j * GROUPS_PER_ROW + (blk * BLOCK + h * HALF) // GROUP + gg
                     nc.vector.tensor_scalar(
-                        out=wt[:, j, col : col + GROUP],
-                        in0=wt[:, j, col : col + GROUP],
-                        scalar1=zp32[:, k : k + 1],
-                        scalar2=sc32[:, k : k + 1],
+                        out=wd[:, j, gg * GROUP : (gg + 1) * GROUP],
+                        in0=wt[:, j, base + gg * GROUP : base + (gg + 1) * GROUP],
+                        scalar1=zp_sb[c][:, k : k + 1],
+                        scalar2=sc_sb[c][:, k : k + 1],
                         op0=ALU.subtract,
                         op1=ALU.mult,
                     )
+            if h == 1 and (blk, c) != (0, 0) and state["loaded"] < len(later_tiles):
+                nxt = later_tiles[state["loaded"]]
+                load_w(nxt[0], nxt[1])
+                state["loaded"] += 1
 
-        def regroup(u, v_cols):
-            ib, c, blk, h = where(u)
-            wt = w_tiles[(blk, c)]
-            base = h * HALF
+        def regroup(n, v_cols):
+            wd = wd_of[n]
             grouped = gpool.tile([P, HALF, PACK], BF16, name="grouped", align_bytes=64)
-            grouped_of[u] = grouped
+            grouped_of[n] = grouped
             nc.vector.tensor_copy(
                 out=grouped[:, 0:v_cols, :].rearrange("p (q i) t -> p q t i", i=4),
-                in_=wt[:, :, base : base + v_cols].rearrange("p t (q i) -> p q t i", i=4),
+                in_=wd[:, :, 0:v_cols].rearrange("p t (q i) -> p q t i", i=4),
             )
             nc.scalar.copy(
                 out=grouped[:, v_cols:HALF, :].rearrange("p (q i) t -> p q t i", i=4),
-                in_=wt[:, :, base + v_cols : base + HALF].rearrange("p t (q i) -> p q t i", i=4),
+                in_=wd[:, :, v_cols:HALF].rearrange("p t (q i) -> p q t i", i=4),
             )
-            if h == 1 and blk + 2 < N_BLOCKS:
-                load_w(blk + 2, c, 0, BLOCK)
 
-        def quantise(u):
+        def quantise(n):
             codes = cpool.tile([P, HALF], U32, name="codes", align_bytes=64)
             scales = cpool.tile([P, HALF], U8, name="scales", align_bytes=64)
-            codes_of[u] = (codes, scales)
+            codes_of[n] = (codes, scales)
             nc.vector.quantize_mx(
                 out=codes[:].bitcast(E4M3X4),
                 scales=scales[:],
-                in_=grouped_of[u][:].rearrange("p w t -> p (w t)"),
+                in_=grouped_of[n][:].rearrange("p w t -> p (w t)"),
             )
-            pending.append(u)
+            pending.append(n)
 
         def multiply_what_can_go():
             while state["multiplied"] < len(pending):
-                u = pending[state["multiplied"]]
-                ib, c, blk, h = where(u)
-                if c >= state["g_ready"]:
+                n = pending[state["multiplied"]]
+                blk, c, h = units[n]
+                ib = 2 * blk + h
+                if state["g_ready"] < N_TT:
                     return
                 if c == 0 and ib >= 2 and evacuated.get(ib - 2, 0) < N_TT:
                     return
                 state["multiplied"] += 1
-                codes, scales = codes_of[u]
+                codes, scales = codes_of[n]
                 for tt in range(N_TT):
                     if c == 0:
                         acc[(ib, tt)] = bank((ib % 2) * N_TT + tt)
-                    lo = (c * N_TT + tt) * P
+                    lo = (tt * N_C + c) * P
                     nc.tensor.matmul_mx(
                         out=acc[(ib, tt)][:],
                         lhsT=g_codes[:, lo : lo + P].bitcast(E5M2X4),
@@ -195,34 +212,34 @@ def tile_qlv4_linear_mod_kernel(
                         stop=(c == N_C - 1),
                     )
 
-        def g_transpose(c):
-            for k in range(2):
-                xt = bank(N_TT + (2 * c + k) % N_TT)
+        def g_transpose(tt):
+            gw = g_sb[tt][:].bitcast(F32).rearrange("p (c m u) -> p c u m", c=N_C, u=2)
+            for ch in range(2):
+                xt = bank(2 * tt + ch)
                 xt_v = xt[:].rearrange("p (a u t) -> p a u t", a=2, u=2)
                 for a in range(2):
-                    gw = g_sb[c][:, 2 * k + a, :].bitcast(F32).rearrange("p (m u) -> p u m", u=2)
                     for u in range(2):
-                        nc.tensor.transpose(xt_v[:, a, u, :], gw[:, u, :], ident[:])
+                        nc.tensor.transpose(xt_v[:, a, u, :], gw[:, 2 * ch + a, u, :], ident[:])
                 gq = qpool.tile([P, 2 * K_PASS], BF16, name="gq", align_bytes=64)
-                gq_of[(c, k)] = gq
+                gq_of[(tt, ch)] = gq
                 nc.scalar.copy(
                     out=gq[:].bitcast(F32).rearrange("p (a t u) -> p a t u", a=2, u=2),
                     in_=xt[:].rearrange("p (a u t) -> p a t u", a=2, u=2),
                 )
 
-        def g_quantise(c):
-            for k in range(2):
-                lo = (c * N_TT + 2 * k) * P
+        def g_quantise(tt):
+            for ch in range(2):
+                lo = (tt * N_C + 2 * ch) * P
                 nc.vector.quantize_mx(
                     out=g_codes[:, lo : lo + 2 * P].bitcast(E5M2X4),
                     scales=g_scales[:, lo : lo + 2 * P],
-                    in_=gq_of[(c, k)][:],
+                    in_=gq_of[(tt, ch)][:],
                 )
-            state["g_ready"] = c + 1
+            state["g_ready"] = tt + 1
 
         def evacuate(ib, tt):
             ev = epool.tile([P, HALF], F32, name="ev")
-            if ib == N_IB - 1 and tt < 2:
+            if ib == N_IB - 1 and tt % 2 == 0:
                 nc.vector.tensor_copy(out=ev[:], in_=acc[(ib, tt)][:])
             else:
                 nc.scalar.copy(out=ev[:], in_=acc[(ib, tt)][:])
@@ -234,18 +251,18 @@ def tile_qlv4_linear_mod_kernel(
         for step in range(N_UNITS + E_LAG):
             if 0 <= step - 2 < N_UNITS:
                 quantise(step - 2)
-            if 0 <= step - G_T0 - 1 < N_C:
-                g_quantise(step - G_T0 - 1)
+            if 0 <= step - G_STEP - 1 < N_TT:
+                g_quantise(step - G_STEP - 1)
             multiply_what_can_go()
             todo = evac_plan.get(step, [])
             if 0 <= step - 1 < N_UNITS:
-                banks_for_scalar = len(todo) + (2 if 0 <= step - G_T0 < N_C else 0)
+                banks_for_scalar = len(todo) + (2 if 0 <= step - G_STEP < N_TT else 0)
                 v_cols = V_COLS[banks_for_scalar]
                 if step - 1 == N_UNITS - 1:
                     v_cols = V_COLS_LAST
                 regroup(step - 1, v_cols)
-            if 0 <= step - G_T0 < N_C:
-                g_transpose(step - G_T0)
+            if 0 <= step - G_STEP < N_TT:
+                g_transpose(step - G_STEP)
             if step < N_UNITS:
                 dequantise(step)
             for ib, tt in todo:

@@ -28,9 +28,10 @@ N_IB = IN_F // HALF
 N_UNITS = N_IB * N_C
 TILE_BY_TILE_BLOCKS = 2
 G_STEP = 5
-E_LAG = 3
+Q_LAG = 3
+E_LAG = 4
 EVAC_LATE = {0: 5, 1: 3}
-V_COLS = {0: 144, 1: 224, 2: 296, 3: 376, 4: 448}
+V_COLS = {0: 128, 1: 208, 2: 280, 3: 360, 4: 432}
 V_COLS_LAST = 256
 
 FLOPS = 2 * TOKENS * OUT_F * IN_F
@@ -72,7 +73,7 @@ def tile_qlv4_linear_mod_kernel(
         const = ctx.enter_context(tc.tile_pool(name="const", bufs=1))
         wpool = ctx.enter_context(tc.tile_pool(name="wq", bufs=8))
         dpool = ctx.enter_context(tc.tile_pool(name="wd", bufs=3))
-        gpool = ctx.enter_context(tc.tile_pool(name="grouped", bufs=4))
+        gpool = ctx.enter_context(tc.tile_pool(name="grouped", bufs=5))
         cpool = ctx.enter_context(tc.tile_pool(name="codes", bufs=16))
         epool = ctx.enter_context(tc.tile_pool(name="ev", bufs=8))
         qpool = ctx.enter_context(tc.tile_pool(name="gq", bufs=4))
@@ -249,8 +250,8 @@ def tile_qlv4_linear_mod_kernel(
             evacuated[ib] = evacuated.get(ib, 0) + 1
 
         for step in range(N_UNITS + E_LAG):
-            if 0 <= step - 2 < N_UNITS:
-                quantise(step - 2)
+            if 0 <= step - Q_LAG < N_UNITS:
+                quantise(step - Q_LAG)
             if 0 <= step - G_STEP - 1 < N_TT:
                 g_quantise(step - G_STEP - 1)
             multiply_what_can_go()

from contextlib import ExitStack

import concourse.mybir as mybir
from concourse.masks import make_identity

F32 = mybir.dt.float32
BF16 = mybir.dt.bfloat16
U32 = mybir.dt.uint32
U8 = mybir.dt.uint8
E4M3X4 = mybir.dt.float8_e4m3fn_x4
E5M2X4 = mybir.dt.float8_e5m2_x4
ALU = mybir.AluOpType

P = 128
PACK = 4
K_PASS = P * PACK
TOKENS = 512
OUT_F = 2048
IN_F = 4096
GROUP = 128
GROUPS_PER_ROW = IN_F // GROUP
N_TT = TOKENS // P
N_C = OUT_F // K_PASS
BLOCK = 1024
HALF = 512
N_BLOCKS = IN_F // BLOCK
N_IB = IN_F // HALF
N_UNITS = N_IB * N_C
TILE_BY_TILE_BLOCKS = 2
G_STEP = 5
Q_LAG = 3
E_LAG = 4
EVAC_LATE = {0: 5, 1: 3}
V_COLS = {0: 128, 1: 208, 2: 280, 3: 360, 4: 432}
V_COLS_LAST = 256

FLOPS = 2 * TOKENS * OUT_F * IN_F
BYTES = 2 * OUT_F * IN_F + 2 * 2 * OUT_F * GROUPS_PER_ROW + 2 * TOKENS * OUT_F + 4 * TOKENS * IN_F


def tile_qlv4_linear_mod_kernel(
    tc, x_in, weight_q, weight_scale, weight_zero_point, grad_out, out
):
    nc = tc.nc
    g2 = grad_out.flatten_outer_dims()
    out2 = out.flatten_outer_dims()
    wq_v = weight_q.rearrange("(c p j) i -> c p j i", p=P, j=PACK)
    sc_v = weight_scale.rearrange("(c p r) one -> c p (r one)", c=N_C, p=P)
    zp_v = weight_zero_point.rearrange("(c p r) one -> c p (r one)", c=N_C, p=P)

    units = []
    for blk in range(N_BLOCKS):
        if blk < TILE_BY_TILE_BLOCKS:
            units.extend([(blk, c, h) for c in range(N_C) for h in range(2)])
        else:
            units.extend([(blk, c, h) for h in range(2) for c in range(N_C)])

    evac_plan = {}
    for ib in range(N_IB):
        close = units.index((ib // 2, N_C - 1, ib % 2))
        for tt in range(N_TT):
            if ib == N_IB - 1:
                step = close + E_LAG
            elif ib // 2 < TILE_BY_TILE_BLOCKS:
                step = close + E_LAG + EVAC_LATE[ib // 2]
            else:
                step = close + E_LAG + tt
            if step not in evac_plan:
                evac_plan[step] = []
            evac_plan[step].append((ib, tt))

    with ExitStack() as ctx:
        const = ctx.enter_context(tc.tile_pool(name="const", bufs=1))
        wpool = ctx.enter_context(tc.tile_pool(name="wq", bufs=8))
        dpool = ctx.enter_context(tc.tile_pool(name="wd", bufs=3))
        gpool = ctx.enter_context(tc.tile_pool(name="grouped", bufs=5))
        cpool = ctx.enter_context(tc.tile_pool(name="codes", bufs=16))
        epool = ctx.enter_context(tc.tile_pool(name="ev", bufs=8))
        qpool = ctx.enter_context(tc.tile_pool(name="gq", bufs=4))
        psum = ctx.enter_context(tc.psum_pool(name="psum", bufs=1))
        ctx.enter_context(tc.manual_schedule())

        def bank(n):
            return psum.tile([P, HALF], F32, name="bank%d" % n, tag="bank%d" % n)

        zp_sb = []
        sc_sb = []

        def load_scalars(c):
            zp_t = const.tile([P, P], BF16, name="zp%d" % c)
            sc_t = const.tile([P, P], BF16, name="sc%d" % c)
            nc.sync.dma_start(out=zp_t[:], in_=zp_v[c])
            nc.sync.dma_start(out=sc_t[:], in_=sc_v[c])
            zp_sb.append(zp_t)
            sc_sb.append(sc_t)

        w_src = {}

        def load_w(blk, c):
            wt = wpool.tile([P, PACK, BLOCK], BF16, name="wt")
            for h in range(2):
                w_src[(blk, c, h)] = (wt, h * HALF)
            nc.sync.dma_start(out=wt[:], in_=wq_v[c][:, :, blk * BLOCK : (blk + 1) * BLOCK])

        g_sb = []

        def load_g(tt):
            g_t = const.tile([P, OUT_F], BF16, name="g_sb%d" % tt)
            nc.sync.dma_start(out=g_t[:], in_=g2[tt * P : (tt + 1) * P, :])
            g_sb.append(g_t)

        load_scalars(0)
        for h in range(2):
            first = const.tile([P, PACK, HALF], BF16, name="first%d" % h)
            w_src[(0, 0, h)] = (first, 0)
            nc.sync.dma_start(out=first[:], in_=wq_v[0][:, :, h * HALF : (h + 1) * HALF])
        load_scalars(1)
        load_w(0, 1)
        load_scalars(2)
        load_w(0, 2)
        load_g(0)
        load_g(1)
        load_scalars(3)
        load_w(0, 3)
        load_g(2)
        load_g(3)
        later_tiles = [(blk, c) for blk in range(1, N_BLOCKS) for c in range(N_C)]
        for blk, c in later_tiles[0:5]:
            load_w(blk, c)
        state = {"g_ready": 0, "multiplied": 0, "loaded": 5}

        ident = const.tile([P, P], F32)
        make_identity(nc, ident[:])

        g_codes = const.tile([P, N_TT * N_C * P], U32, align_bytes=64)
        g_scales = const.tile([P, N_TT * N_C * P], U8, align_bytes=64)

        wd_of = {}
        grouped_of = {}
        codes_of = {}
        gq_of = {}
        acc = {}
        evacuated = {}
        pending = []

        def dequantise(n):
            blk, c, h = units[n]
            wt, base = w_src[(blk, c, h)]
            wd = dpool.tile([P, PACK, HALF], BF16, name="wd")
            wd_of[n] = wd
            for j in range(PACK):
                for gg in range(HALF // GROUP):
                    k = j * GROUPS_PER_ROW + (blk * BLOCK + h * HALF) // GROUP + gg
                    nc.vector.tensor_scalar(
                        out=wd[:, j, gg * GROUP : (gg + 1) * GROUP],
                        in0=wt[:, j, base + gg * GROUP : base + (gg + 1) * GROUP],
                        scalar1=zp_sb[c][:, k : k + 1],
                        scalar2=sc_sb[c][:, k : k + 1],
                        op0=ALU.subtract,
                        op1=ALU.mult,
                    )
            if h == 1 and (blk, c) != (0, 0) and state["loaded"] < len(later_tiles):
                nxt = later_tiles[state["loaded"]]
                load_w(nxt[0], nxt[1])
                state["loaded"] += 1

        def regroup(n, v_cols):
            wd = wd_of[n]
            grouped = gpool.tile([P, HALF, PACK], BF16, name="grouped", align_bytes=64)
            grouped_of[n] = grouped
            nc.vector.tensor_copy(
                out=grouped[:, 0:v_cols, :].rearrange("p (q i) t -> p q t i", i=4),
                in_=wd[:, :, 0:v_cols].rearrange("p t (q i) -> p q t i", i=4),
            )
            nc.scalar.copy(
                out=grouped[:, v_cols:HALF, :].rearrange("p (q i) t -> p q t i", i=4),
                in_=wd[:, :, v_cols:HALF].rearrange("p t (q i) -> p q t i", i=4),
            )

        def quantise(n):
            codes = cpool.tile([P, HALF], U32, name="codes", align_bytes=64)
            scales = cpool.tile([P, HALF], U8, name="scales", align_bytes=64)
            codes_of[n] = (codes, scales)
            nc.vector.quantize_mx(
                out=codes[:].bitcast(E4M3X4),
                scales=scales[:],
                in_=grouped_of[n][:].rearrange("p w t -> p (w t)"),
            )
            pending.append(n)

        def multiply_what_can_go():
            while state["multiplied"] < len(pending):
                n = pending[state["multiplied"]]
                blk, c, h = units[n]
                ib = 2 * blk + h
                if state["g_ready"] < N_TT:
                    return
                if c == 0 and ib >= 2 and evacuated.get(ib - 2, 0) < N_TT:
                    return
                state["multiplied"] += 1
                codes, scales = codes_of[n]
                for tt in range(N_TT):
                    if c == 0:
                        acc[(ib, tt)] = bank((ib % 2) * N_TT + tt)
                    lo = (tt * N_C + c) * P
                    nc.tensor.matmul_mx(
                        out=acc[(ib, tt)][:],
                        lhsT=g_codes[:, lo : lo + P].bitcast(E5M2X4),
                        lhsT_scale=g_scales[:, lo : lo + P],
                        rhs=codes[:].bitcast(E4M3X4),
                        rhs_scale=scales[:],
                        start=(c == 0),
                        stop=(c == N_C - 1),
                    )

        def g_transpose(tt):
            gw = g_sb[tt][:].bitcast(F32).rearrange("p (c m u) -> p c u m", c=N_C, u=2)
            for ch in range(2):
                xt = bank(2 * tt + ch)
                xt_v = xt[:].rearrange("p (a u t) -> p a u t", a=2, u=2)
                for a in range(2):
                    for u in range(2):
                        nc.tensor.transpose(xt_v[:, a, u, :], gw[:, 2 * ch + a, u, :], ident[:])
                gq = qpool.tile([P, 2 * K_PASS], BF16, name="gq", align_bytes=64)
                gq_of[(tt, ch)] = gq
                nc.scalar.copy(
                    out=gq[:].bitcast(F32).rearrange("p (a t u) -> p a t u", a=2, u=2),
                    in_=xt[:].rearrange("p (a u t) -> p a t u", a=2, u=2),
                )

        def g_quantise(tt):
            for ch in range(2):
                lo = (tt * N_C + 2 * ch) * P
                nc.vector.quantize_mx(
                    out=g_codes[:, lo : lo + 2 * P].bitcast(E5M2X4),
                    scales=g_scales[:, lo : lo + 2 * P],
                    in_=gq_of[(tt, ch)][:],
                )
            state["g_ready"] = tt + 1

        def evacuate(ib, tt):
            ev = epool.tile([P, HALF], F32, name="ev")
            if ib == N_IB - 1 and tt % 2 == 0:
                nc.vector.tensor_copy(out=ev[:], in_=acc[(ib, tt)][:])
            else:
                nc.scalar.copy(out=ev[:], in_=acc[(ib, tt)][:])
            nc.sync.dma_start(
                out=out2[tt * P : (tt + 1) * P, ib * HALF : (ib + 1) * HALF], in_=ev[:]
            )
            evacuated[ib] = evacuated.get(ib, 0) + 1

        for step in range(N_UNITS + E_LAG):
            if 0 <= step - Q_LAG < N_UNITS:
                quantise(step - Q_LAG)
            if 0 <= step - G_STEP - 1 < N_TT:
                g_quantise(step - G_STEP - 1)
            multiply_what_can_go()
            todo = evac_plan.get(step, [])
            if 0 <= step - 1 < N_UNITS:
                banks_for_scalar = len(todo) + (2 if 0 <= step - G_STEP < N_TT else 0)
                v_cols = V_COLS[banks_for_scalar]
                if step - 1 == N_UNITS - 1:
                    v_cols = V_COLS_LAST
                regroup(step - 1, v_cols)
            if 0 <= step - G_STEP < N_TT:
                g_transpose(step - G_STEP)
            if step < N_UNITS:
                dequantise(step)
            for ib, tt in todo:
                evacuate(ib, tt)
            multiply_what_can_go()
